import numpy as np
import ml_dtypes


def mxq(x, axis, fmt="e4m3"):
    dtype, down = {"e4m3": (ml_dtypes.float8_e4m3fn, 7), "e5m2": (ml_dtypes.float8_e5m2, 14)}[fmt]
    v = np.moveaxis(np.asarray(x, np.float32).astype(ml_dtypes.bfloat16).astype(np.float64), axis, -1)
    blocks = v.reshape(v.shape[:-1] + (-1, 32))
    amax = np.abs(blocks).max(-1, keepdims=True)
    byte = np.maximum(np.where(amax > 0, np.frexp(amax)[1] - 1 + 127, 0) - down, 1)
    scale = np.exp2(byte - 127.0)
    codes = (blocks / scale).astype(np.float32).astype(dtype).astype(np.float64)
    return np.moveaxis((codes * scale).reshape(v.shape), -1, axis)


WIDE = False


def mx_kscale(k):
    if not WIDE:
        return np.ones(k)
    levels = np.array([10, -10, 5, -5, 0])
    a = np.random.permutation(np.resize(levels, k // 512 * 4)).reshape(k // 512, 4)
    idx = np.arange(k)
    return np.exp2(a[idx // 512, idx % 128 // 32])


BF16 = ml_dtypes.bfloat16


def bf(x):
    return np.asarray(x, np.float32).astype(BF16)


def f64(x):
    return np.asarray(x).astype(np.float64)


E2M1 = np.array([0.0, 0.5, 1.0, 1.5, 2.0, 3.0, 4.0, 6.0, -0.0, -0.5, -1.0, -1.5, -2.0, -3.0, -4.0, -6.0])


def pack_weight(w, fmt):
    k, n = w.shape
    w = f64(bf(w)).reshape(k // 32, 32, n)
    amax = np.abs(w).max(1)
    if fmt == "e4m3":
        byte = np.frexp(amax)[1] - 1 + 127 - 7
    else:
        mant, ex = np.frexp(amax / 6.0)
        byte = np.where(mant > 0.5, ex, ex - 1) + 127
    byte = np.clip(np.where(amax > 0, byte, 1), 1, 254)
    scaled = (w * np.exp2(127.0 - byte)[:, None, :]).reshape(k, n).astype(np.float32)
    by_word = np.ascontiguousarray(scaled.reshape(k // 512, 128, 4, n).transpose(0, 1, 3, 2))
    if fmt == "e4m3":
        words = by_word.astype(ml_dtypes.float8_e4m3fn).view(np.uint8)
    else:
        c = by_word.astype(ml_dtypes.float4_e2m1fn).view(np.uint8) & 0xF
        words = c[..., 0::2] | (c[..., 1::2] << 4)
    return np.ascontiguousarray(words), np.ascontiguousarray(byte.astype(np.uint8).reshape(k // 512, 16, n))


def unpack_weight(words, scales, fmt):
    g, p, n, _ = words.shape
    if fmt == "e4m3":
        vals = np.ascontiguousarray(words).view(ml_dtypes.float8_e4m3fn).astype(np.float64)
    else:
        nib = np.empty((g, p, n, 4), np.uint8)
        nib[..., 0::2] = words & 0xF
        nib[..., 1::2] = words >> 4
        vals = E2M1[nib]
    vals = vals * np.repeat(np.exp2(scales.astype(np.float64) - 127.0), 8, axis=1)[..., None]
    return vals.transpose(0, 1, 3, 2).reshape(g * 512, n)

def pack4(w):
    words, scales = pack_weight(w, "e2m1")
    return words.reshape(words.shape[0], 128, -1), scales


def unpack4(words, scales):
    return unpack_weight(words.reshape(words.shape[0], 128, -1, 2), scales, "e2m1")


B, T, C, H = 4, 128, 2048, 32
HD = C // H


def rotary_pos_emb(v):
    exponents = f64(np.arange(0, HD, 2)[: HD // 2] // HD)
    freqs = 1.0 / np.power(1000.0, exponents)
    theta = f64(np.arange(T))[:, None] * freqs[None, :]
    cos = np.cos(theta)[None, :, None, :]
    sin = np.sin(theta)[None, :, None, :]
    vr = v.reshape(B, T, H, HD // 2, 2)
    v0, v1 = vr[..., 0], vr[..., 1]
    out = np.stack([v0 * cos - v1 * sin, v0 * sin + v1 * cos], axis=-1)
    return out.reshape(B, T, H, HD)


def setup_inputs():
    s = mx_kscale(C)
    x = bf(np.random.standard_normal((B, T, C)) * s)
    wq = np.random.standard_normal((C, C)) / np.sqrt(C) / s[None, :]
    wk = np.random.standard_normal((C, C)) / np.sqrt(C) / s[None, :]
    wq_words, wq_scales = pack4(np.ascontiguousarray(wq.T))
    wk_words, wk_scales = pack4(np.ascontiguousarray(wk.T))
    return {"x": x,
            "wq_words": wq_words, "wq_scales": wq_scales,
            "wk_words": wk_words, "wk_scales": wk_scales}


def reference(x, wq_words, wq_scales, wk_words, wk_scales):
    xm = mxq(f64(x), 2, "e4m3")
    q = (xm @ unpack4(wq_words, wq_scales)).reshape(B, T, H, HD)
    k = (xm @ unpack4(wk_words, wk_scales)).reshape(B, T, H, HD)
    return rotary_pos_emb(q), rotary_pos_emb(k)

@@ -1,0 +1,199 @@
+import math
+from contextlib import ExitStack
+
+import concourse.mybir as mybir
+from concourse.masks import make_identity
+
+F32 = mybir.dt.float32
+BF16 = mybir.dt.bfloat16
+I32 = mybir.dt.int32
+U32 = mybir.dt.uint32
+U8 = mybir.dt.uint8
+FP8X4 = mybir.dt.float8_e4m3fn_x4
+FP4X4 = mybir.dt.float4_e2m1fn_x4
+ALU = mybir.AluOpType
+ACT = mybir.ActivationFunctionType
+
+P = 128
+BATCHES = 4
+CHANNELS = 2048
+PACK = 4
+K_PASS = P * PACK
+PASSES = CHANNELS // K_PASS
+N_CHUNK = 512
+CHUNKS = CHANNELS // N_CHUNK
+PSUM_BANKS = 8
+SCALE_ROWS = 4
+
+FLOPS = 2 * 2 * BATCHES * P * CHANNELS * CHANNELS
+
+TWO_PI_HIGH = 6.28125
+TWO_PI_LOW = 2.0 * math.pi - TWO_PI_HIGH
+ROUND_TO_WHOLE = 1.5 * 2.0**23
+
+
+def load_weight_chunk(nc, pool, words_dram, scales_dram, j, label):
+    words = pool.tile(
+        [P, PASSES, 2 * N_CHUNK], U8, name="words_" + label, tag="words_" + label, align_bytes=64
+    )
+    planes = pool.tile(
+        [P, PASSES, N_CHUNK], U8, name="planes_" + label, tag="planes_" + label, align_bytes=64
+    )
+    nc.vector.memset(planes[:].bitcast(I32), 0)
+    byte_cols = slice(2 * N_CHUNK * j, 2 * N_CHUNK * (j + 1))
+    nc.sync.dma_start(
+        out=words[:].bitcast(I32),
+        in_=words_dram[:, :, byte_cols].rearrange("g p c -> p g c").bitcast(I32),
+    )
+    n_cols = slice(N_CHUNK * j, N_CHUNK * (j + 1))
+    for r in range(SCALE_ROWS):
+        nc.sync.dma_start(
+            out=planes[r:P:32].bitcast(I32),
+            in_=scales_dram[:, r : 4 * SCALE_ROWS : SCALE_ROWS, n_cols]
+            .rearrange("g q n -> q g n")
+            .bitcast(I32),
+        )
+    return words, planes
+
+
+def rotation_factors(nc, pool, position):
+    angle = pool.tile([P, 1], F32, name="angle")
+    turns = pool.tile([P, 1], F32, name="turns")
+    quarter_less = pool.tile([P, 1], F32, name="quarter_less")
+    cos_t = pool.tile([P, 1], F32, name="cos_t")
+    sin_t = pool.tile([P, 1], F32, name="sin_t")
+    neg_sin_t = pool.tile([P, 1], F32, name="neg_sin_t")
+
+    nc.vector.tensor_copy(out=angle[:], in_=position[:])
+    nc.vector.tensor_scalar(
+        out=turns[:], in0=angle[:], scalar1=1.0 / (2.0 * math.pi), scalar2=ROUND_TO_WHOLE,
+        op0=ALU.mult, op1=ALU.add,
+    )
+    nc.vector.tensor_scalar(
+        out=turns[:], in0=turns[:], scalar1=ROUND_TO_WHOLE, scalar2=None, op0=ALU.subtract
+    )
+    for part in (TWO_PI_HIGH, TWO_PI_LOW):
+        nc.vector.scalar_tensor_tensor(
+            out=angle[:], in0=turns[:], scalar=-part, in1=angle[:], op0=ALU.mult, op1=ALU.add
+        )
+    nc.vector.scalar_tensor_tensor(
+        out=quarter_less[:], in0=angle[:], scalar=-1.0, in1=angle[:], op0=ALU.mult, op1=ALU.min
+    )
+    nc.vector.tensor_scalar(
+        out=quarter_less[:], in0=quarter_less[:], scalar1=0.5 * math.pi, scalar2=None, op0=ALU.add
+    )
+    nc.scalar.activation(out=sin_t[:], in_=angle[:], func=ACT.Sin)
+    nc.scalar.activation(out=neg_sin_t[:], in_=angle[:], func=ACT.Sin, scale=-1.0)
+    nc.scalar.activation(out=cos_t[:], in_=quarter_less[:], func=ACT.Sin)
+    return cos_t, sin_t, neg_sin_t
+
+
+def quantise_batch(nc, pool, psum, x_rows, identity, label):
+    x_words = x_rows[:].bitcast(F32)
+    grouped = pool.tile(
+        [P, PASSES, P, PACK], BF16, name="grouped_" + label, tag="grouped_" + label, align_bytes=64
+    )
+    grouped_words = grouped[:].bitcast(F32)
+    words_per_pass = K_PASS // 2
+    for first_pass in range(0, PASSES, 2):
+        flipped = psum.tile([P, 2, 2, P], F32, name="flipped", tag="bank")
+        for s in range(2):
+            for u in range(2):
+                start = words_per_pass * (first_pass + s)
+                nc.tensor.transpose(
+                    flipped[:, s, u, :],
+                    x_words[:, start + u : start + words_per_pass : 2],
+                    identity[:],
+                )
+        copy_out = nc.vector.tensor_copy if first_pass == 0 else nc.scalar.copy
+        copy_out(
+            out=grouped_words[:, first_pass : first_pass + 2, :, :],
+            in_=flipped[:].rearrange("p s u r -> p s r u"),
+        )
+    codes = pool.tile(
+        [P, PASSES * P], U32, name="codes_" + label, tag="codes_" + label, align_bytes=64
+    )
+    plane = pool.tile(
+        [P, PASSES * P], U8, name="plane_" + label, tag="plane_" + label, align_bytes=64
+    )
+    nc.vector.quantize_mx(
+        out=codes[:].bitcast(FP8X4),
+        scales=plane[:],
+        in_=grouped[:].rearrange("p g r t -> p (g r t)"),
+    )
+    return codes, plane
+
+
+def tile_attention_pa_kernel(
+    tc, x, wq_words, wq_scales, wk_words, wk_scales, out_0, out_1
+):
+    nc = tc.nc
+    with ExitStack() as ctx:
+        resident = ctx.enter_context(tc.tile_pool(name="resident", bufs=1))
+        turned_pool = ctx.enter_context(tc.tile_pool(name="turned", bufs=3))
+        result_pool = ctx.enter_context(tc.tile_pool(name="result", bufs=8))
+        psum = ctx.enter_context(tc.psum_pool(name="psum", bufs=PSUM_BANKS))
+        ctx.enter_context(tc.manual_schedule())
+
+        position = resident.tile([P, 1], I32, name="position")
+        nc.gpsimd.iota(position[:], pattern=[[0, 1]], base=0, channel_multiplier=1)
+        identity = resident.tile([P, P], F32, name="identity")
+        make_identity(nc, identity[:])
+
+        x_rows = []
+        for b in range(BATCHES):
+            rows = resident.tile([P, CHANNELS], BF16, name="x_rows_%d" % b, tag="x_rows_%d" % b)
+            nc.sync.dma_start(out=rows[:], in_=x[b])
+            x_rows.append(rows)
+        chunks = []
+        for name, words_dram, scales_dram, out_dram in (
+            ("q", wq_words, wq_scales, out_0),
+            ("k", wk_words, wk_scales, out_1),
+        ):
+            out_rows = out_dram.rearrange("b t h d -> b t (h d)")
+            for j in range(CHUNKS):
+                words, planes = load_weight_chunk(
+                    nc, resident, words_dram, scales_dram, j, "%s%d" % (name, j)
+                )
+                chunks.append((words, planes, out_rows[:, :, N_CHUNK * j : N_CHUNK * (j + 1)]))
+
+        cos_t, sin_t, neg_sin_t = rotation_factors(nc, resident, position)
+
+        x_mx = [
+            quantise_batch(nc, resident, psum, x_rows[b], identity, "%d" % b)
+            for b in range(BATCHES)
+        ]
+
+        for words, planes, out_cols in chunks:
+            for b in range(BATCHES):
+                codes, plane = x_mx[b]
+                sums = psum.tile([P, N_CHUNK], F32, name="sums", tag="bank")
+                for g in range(PASSES):
+                    positions = slice(P * g, P * (g + 1))
+                    nc.tensor.matmul_mx(
+                        out=sums[:],
+                        lhsT=codes[:, positions].bitcast(FP8X4),
+                        lhsT_scale=plane[:, positions],
+                        rhs=words[:, g, :].bitcast(FP4X4),
+                        rhs_scale=planes[:, g, :],
+                        start=(g == 0),
+                        stop=(g == PASSES - 1),
+                    )
+                pairs = sums[:].rearrange("p (i e) -> p i e", e=2)
+                turned = turned_pool.tile([P, 2, N_CHUNK // 2], F32, name="turned")
+                nc.scalar.activation(
+                    out=turned[:, 0, :], in_=pairs[:, :, 1], func=ACT.Copy, scale=neg_sin_t[:]
+                )
+                nc.scalar.activation(
+                    out=turned[:, 1, :], in_=pairs[:, :, 0], func=ACT.Copy, scale=sin_t[:]
+                )
+                result = result_pool.tile([P, N_CHUNK], F32, name="result")
+                nc.vector.scalar_tensor_tensor(
+                    out=result[:].rearrange("p (i e) -> p i e", e=2),
+                    in0=pairs,
+                    scalar=cos_t[:],
+                    in1=turned[:].rearrange("p e i -> p i e"),
+                    op0=ALU.mult,
+                    op1=ALU.add,
+                )
+                nc.sync.dma_start(out=out_cols[b], in_=result[:])

@@ -133,7 +133,6 @@ def tile_attention_pa_kernel(
         turned_pool = ctx.enter_context(tc.tile_pool(name="turned", bufs=3))
         result_pool = ctx.enter_context(tc.tile_pool(name="result", bufs=8))
         psum = ctx.enter_context(tc.psum_pool(name="psum", bufs=PSUM_BANKS))
-        ctx.enter_context(tc.manual_schedule())
 
         position = resident.tile([P, 1], I32, name="position")
         nc.gpsimd.iota(position[:], pattern=[[0, 1]], base=0, channel_multiplier=1)

@@ -21,9 +21,11 @@ PACK = 4
 K_PASS = P * PACK
 PASSES = CHANNELS // K_PASS
 N_CHUNK = 512
+N_LAST = 128
 CHUNKS = CHANNELS // N_CHUNK
 PSUM_BANKS = 8
-SCALE_ROWS = 4
+QUADRANT = 32
+SCALE_ROWS = QUADRANT // 8
 
 FLOPS = 2 * 2 * BATCHES * P * CHANNELS * CHANNELS
 
@@ -33,26 +35,27 @@ ROUND_TO_WHOLE = 1.5 * 2.0**23
 
 
 def load_weight_chunk(nc, pool, words_dram, scales_dram, j, label):
-    words = pool.tile(
-        [P, PASSES, 2 * N_CHUNK], U8, name="words_" + label, tag="words_" + label, align_bytes=64
-    )
     planes = pool.tile(
         [P, PASSES, N_CHUNK], U8, name="planes_" + label, tag="planes_" + label, align_bytes=64
     )
     nc.vector.memset(planes[:].bitcast(I32), 0)
-    byte_cols = slice(2 * N_CHUNK * j, 2 * N_CHUNK * (j + 1))
-    nc.sync.dma_start(
-        out=words[:].bitcast(I32),
-        in_=words_dram[:, :, byte_cols].rearrange("g p c -> p g c").bitcast(I32),
-    )
     n_cols = slice(N_CHUNK * j, N_CHUNK * (j + 1))
     for r in range(SCALE_ROWS):
         nc.sync.dma_start(
-            out=planes[r:P:32].bitcast(I32),
-            in_=scales_dram[:, r : 4 * SCALE_ROWS : SCALE_ROWS, n_cols]
+            out=planes[r:P:QUADRANT].bitcast(I32),
+            in_=scales_dram[:, r : P // 8 : SCALE_ROWS, n_cols]
             .rearrange("g q n -> q g n")
             .bitcast(I32),
         )
+    byte_cols = slice(2 * N_CHUNK * j, 2 * N_CHUNK * (j + 1))
+    words = []
+    for g in range(PASSES):
+        pass_label = "words_%s_%d" % (label, g)
+        pass_words = pool.tile([P, 2 * N_CHUNK], U8, name=pass_label, tag=pass_label, align_bytes=64)
+        nc.sync.dma_start(
+            out=pass_words[:].bitcast(I32), in_=words_dram[g, :, byte_cols].bitcast(I32)
+        )
+        words.append(pass_words)
     return words, planes
 
 
@@ -133,6 +136,7 @@ def tile_attention_pa_kernel(
         turned_pool = ctx.enter_context(tc.tile_pool(name="turned", bufs=3))
         result_pool = ctx.enter_context(tc.tile_pool(name="result", bufs=8))
         psum = ctx.enter_context(tc.psum_pool(name="psum", bufs=PSUM_BANKS))
+        ctx.enter_context(tc.manual_schedule())
 
         position = resident.tile([P, 1], I32, name="position")
         nc.gpsimd.iota(position[:], pattern=[[0, 1]], base=0, channel_multiplier=1)
@@ -163,36 +167,42 @@ def tile_attention_pa_kernel(
             for b in range(BATCHES)
         ]
 
-        for words, planes, out_cols in chunks:
+        def project_and_turn(b, words, planes, out_cols, first, width):
+            codes, plane = x_mx[b]
+            sums = psum.tile([P, width], F32, name="sums", tag="bank")
+            for g in range(PASSES):
+                positions = slice(P * g, P * (g + 1))
+                nc.tensor.matmul_mx(
+                    out=sums[:],
+                    lhsT=codes[:, positions].bitcast(FP8X4),
+                    lhsT_scale=plane[:, positions],
+                    rhs=words[g][:, 2 * first : 2 * (first + width)].bitcast(FP4X4),
+                    rhs_scale=planes[:, g, first : first + width],
+                    start=(g == 0),
+                    stop=(g == PASSES - 1),
+                )
+            pairs = sums[:].rearrange("p (i e) -> p i e", e=2)
+            turned = turned_pool.tile([P, 2, width // 2], F32, name="turned")
+            nc.scalar.activation(
+                out=turned[:, 0, :], in_=pairs[:, :, 1], func=ACT.Copy, scale=neg_sin_t[:]
+            )
+            nc.scalar.activation(
+                out=turned[:, 1, :], in_=pairs[:, :, 0], func=ACT.Copy, scale=sin_t[:]
+            )
+            result = result_pool.tile([P, width], F32, name="result")
+            nc.vector.scalar_tensor_tensor(
+                out=result[:].rearrange("p (i e) -> p i e", e=2),
+                in0=pairs,
+                scalar=cos_t[:],
+                in1=turned[:].rearrange("p e i -> p i e"),
+                op0=ALU.mult,
+                op1=ALU.add,
+            )
+            nc.sync.dma_start(out=out_cols[b, :, first : first + width], in_=result[:])
+
+        last_bank = (len(chunks) - 1, BATCHES - 1)
+        for c, (words, planes, out_cols) in enumerate(chunks):
             for b in range(BATCHES):
-                codes, plane = x_mx[b]
-                sums = psum.tile([P, N_CHUNK], F32, name="sums", tag="bank")
-                for g in range(PASSES):
-                    positions = slice(P * g, P * (g + 1))
-                    nc.tensor.matmul_mx(
-                        out=sums[:],
-                        lhsT=codes[:, positions].bitcast(FP8X4),
-                        lhsT_scale=plane[:, positions],
-                        rhs=words[:, g, :].bitcast(FP4X4),
-                        rhs_scale=planes[:, g, :],
-                        start=(g == 0),
-                        stop=(g == PASSES - 1),
-                    )
-                pairs = sums[:].rearrange("p (i e) -> p i e", e=2)
-                turned = turned_pool.tile([P, 2, N_CHUNK // 2], F32, name="turned")
-                nc.scalar.activation(
-                    out=turned[:, 0, :], in_=pairs[:, :, 1], func=ACT.Copy, scale=neg_sin_t[:]
-                )
-                nc.scalar.activation(
-                    out=turned[:, 1, :], in_=pairs[:, :, 0], func=ACT.Copy, scale=sin_t[:]
-                )
-                result = result_pool.tile([P, N_CHUNK], F32, name="result")
-                nc.vector.scalar_tensor_tensor(
-                    out=result[:].rearrange("p (i e) -> p i e", e=2),
-                    in0=pairs,
-                    scalar=cos_t[:],
-                    in1=turned[:].rearrange("p e i -> p i e"),
-                    op0=ALU.mult,
-                    op1=ALU.add,
-                )
-                nc.sync.dma_start(out=out_cols[b], in_=result[:])
+                width = N_LAST if (c, b) == last_bank else N_CHUNK
+                for first in range(0, N_CHUNK, width):
+                    project_and_turn(b, words, planes, out_cols, first, width)

@@ -24,6 +24,7 @@ N_CHUNK = 512
 N_LAST = 128
 CHUNKS = CHANNELS // N_CHUNK
 PSUM_BANKS = 8
+CHUNKS_AHEAD = 2
 QUADRANT = 32
 SCALE_ROWS = QUADRANT // 8
 
@@ -148,17 +149,20 @@ def tile_attention_pa_kernel(
             rows = resident.tile([P, CHANNELS], BF16, name="x_rows_%d" % b, tag="x_rows_%d" % b)
             nc.sync.dma_start(out=rows[:], in_=x[b])
             x_rows.append(rows)
-        chunks = []
-        for name, words_dram, scales_dram, out_dram in (
-            ("q", wq_words, wq_scales, out_0),
-            ("k", wk_words, wk_scales, out_1),
-        ):
-            out_rows = out_dram.rearrange("b t h d -> b t (h d)")
-            for j in range(CHUNKS):
-                words, planes = load_weight_chunk(
-                    nc, resident, words_dram, scales_dram, j, "%s%d" % (name, j)
-                )
-                chunks.append((words, planes, out_rows[:, :, N_CHUNK * j : N_CHUNK * (j + 1)]))
+        sources = [
+            (words_dram, scales_dram, j, "%s%d" % (name, j))
+            for name, words_dram, scales_dram in (
+                ("q", wq_words, wq_scales),
+                ("k", wk_words, wk_scales),
+            )
+            for j in range(CHUNKS)
+        ]
+        targets = [
+            out_dram.rearrange("b t h d -> b t (h d)")[:, :, N_CHUNK * j : N_CHUNK * (j + 1)]
+            for out_dram in (out_0, out_1)
+            for j in range(CHUNKS)
+        ]
+        chunks = [load_weight_chunk(nc, resident, *sources[c]) for c in range(CHUNKS_AHEAD)]
 
         cos_t, sin_t, neg_sin_t = rotation_factors(nc, resident, position)
 
@@ -200,9 +204,12 @@ def tile_attention_pa_kernel(
             )
             nc.sync.dma_start(out=out_cols[b, :, first : first + width], in_=result[:])
 
-        last_bank = (len(chunks) - 1, BATCHES - 1)
-        for c, (words, planes, out_cols) in enumerate(chunks):
+        last_bank = (len(sources) - 1, BATCHES - 1)
+        for c in range(len(sources)):
+            if c + CHUNKS_AHEAD < len(sources):
+                chunks.append(load_weight_chunk(nc, resident, *sources[c + CHUNKS_AHEAD]))
+            words, planes = chunks[c]
             for b in range(BATCHES):
                 width = N_LAST if (c, b) == last_bank else N_CHUNK
                 for first in range(0, N_CHUNK, width):
-                    project_and_turn(b, words, planes, out_cols, first, width)
+                    project_and_turn(b, words, planes, targets[c], first, width)

@@ -35,7 +35,7 @@ TWO_PI_LOW = 2.0 * math.pi - TWO_PI_HIGH
 ROUND_TO_WHOLE = 1.5 * 2.0**23
 
 
-def load_weight_chunk(nc, pool, words_dram, scales_dram, j, label):
+def load_chunk_scales(nc, pool, words_dram, scales_dram, j, label):
     planes = pool.tile(
         [P, PASSES, N_CHUNK], U8, name="planes_" + label, tag="planes_" + label, align_bytes=64
     )
@@ -48,6 +48,10 @@ def load_weight_chunk(nc, pool, words_dram, scales_dram, j, label):
             .rearrange("g q n -> q g n")
             .bitcast(I32),
         )
+    return planes
+
+
+def load_chunk_words(nc, pool, words_dram, scales_dram, j, label):
     byte_cols = slice(2 * N_CHUNK * j, 2 * N_CHUNK * (j + 1))
     words = []
     for g in range(PASSES):
@@ -57,6 +61,12 @@ def load_weight_chunk(nc, pool, words_dram, scales_dram, j, label):
             out=pass_words[:].bitcast(I32), in_=words_dram[g, :, byte_cols].bitcast(I32)
         )
         words.append(pass_words)
+    return words
+
+
+def load_weight_chunk(nc, pool, words_dram, scales_dram, j, label):
+    planes = load_chunk_scales(nc, pool, words_dram, scales_dram, j, label)
+    words = load_chunk_words(nc, pool, words_dram, scales_dram, j, label)
     return words, planes
 
 
@@ -144,11 +154,6 @@ def tile_attention_pa_kernel(
         identity = resident.tile([P, P], F32, name="identity")
         make_identity(nc, identity[:])
 
-        x_rows = []
-        for b in range(BATCHES):
-            rows = resident.tile([P, CHANNELS], BF16, name="x_rows_%d" % b, tag="x_rows_%d" % b)
-            nc.sync.dma_start(out=rows[:], in_=x[b])
-            x_rows.append(rows)
         sources = [
             (words_dram, scales_dram, j, "%s%d" % (name, j))
             for name, words_dram, scales_dram in (
@@ -162,7 +167,14 @@ def tile_attention_pa_kernel(
             for out_dram in (out_0, out_1)
             for j in range(CHUNKS)
         ]
-        chunks = [load_weight_chunk(nc, resident, *sources[c]) for c in range(CHUNKS_AHEAD)]
+        first_planes = load_chunk_scales(nc, resident, *sources[0])
+        x_rows = []
+        for b in range(BATCHES):
+            rows = resident.tile([P, CHANNELS], BF16, name="x_rows_%d" % b, tag="x_rows_%d" % b)
+            nc.sync.dma_start(out=rows[:], in_=x[b])
+            x_rows.append(rows)
+        chunks = [(load_chunk_words(nc, resident, *sources[0]), first_planes)]
+        chunks.extend([load_weight_chunk(nc, resident, *sources[c]) for c in range(1, CHUNKS_AHEAD)])
 
         cos_t, sin_t, neg_sin_t = rotation_factors(nc, resident, position)
 

@@ -167,12 +167,13 @@ def tile_attention_pa_kernel(
             for out_dram in (out_0, out_1)
             for j in range(CHUNKS)
         ]
-        first_planes = load_chunk_scales(nc, resident, *sources[0])
         x_rows = []
         for b in range(BATCHES):
             rows = resident.tile([P, CHANNELS], BF16, name="x_rows_%d" % b, tag="x_rows_%d" % b)
             nc.sync.dma_start(out=rows[:], in_=x[b])
             x_rows.append(rows)
+            if b == 0:
+                first_planes = load_chunk_scales(nc, resident, *sources[0])
         chunks = [(load_chunk_words(nc, resident, *sources[0]), first_planes)]
         chunks.extend([load_weight_chunk(nc, resident, *sources[c]) for c in range(1, CHUNKS_AHEAD)])
 

@@ -24,7 +24,7 @@ N_CHUNK = 512
 N_LAST = 128
 CHUNKS = CHANNELS // N_CHUNK
 PSUM_BANKS = 8
-CHUNKS_AHEAD = 2
+CHUNKS_AHEAD = 3
 QUADRANT = 32
 SCALE_ROWS = QUADRANT // 8
 

@@ -35,11 +35,15 @@ TWO_PI_LOW = 2.0 * math.pi - TWO_PI_HIGH
 ROUND_TO_WHOLE = 1.5 * 2.0**23
 
 
-def load_chunk_scales(nc, pool, words_dram, scales_dram, j, label):
+def blank_planes(nc, pool, memset, label):
     planes = pool.tile(
         [P, PASSES, N_CHUNK], U8, name="planes_" + label, tag="planes_" + label, align_bytes=64
     )
-    nc.vector.memset(planes[:].bitcast(I32), 0)
+    memset(planes[:].bitcast(I32), 0)
+    return planes
+
+
+def load_chunk_scales(nc, planes, words_dram, scales_dram, j, label):
     n_cols = slice(N_CHUNK * j, N_CHUNK * (j + 1))
     for r in range(SCALE_ROWS):
         nc.sync.dma_start(
@@ -48,7 +52,6 @@ def load_chunk_scales(nc, pool, words_dram, scales_dram, j, label):
             .rearrange("g q n -> q g n")
             .bitcast(I32),
         )
-    return planes
 
 
 def load_chunk_words(nc, pool, words_dram, scales_dram, j, label):
@@ -64,10 +67,9 @@ def load_chunk_words(nc, pool, words_dram, scales_dram, j, label):
     return words
 
 
-def load_weight_chunk(nc, pool, words_dram, scales_dram, j, label):
-    planes = load_chunk_scales(nc, pool, words_dram, scales_dram, j, label)
-    words = load_chunk_words(nc, pool, words_dram, scales_dram, j, label)
-    return words, planes
+def load_weight_chunk(nc, pool, planes, words_dram, scales_dram, j, label):
+    load_chunk_scales(nc, planes, words_dram, scales_dram, j, label)
+    return load_chunk_words(nc, pool, words_dram, scales_dram, j, label)
 
 
 def rotation_factors(nc, pool, position):
@@ -144,7 +146,7 @@ def tile_attention_pa_kernel(
     nc = tc.nc
     with ExitStack() as ctx:
         resident = ctx.enter_context(tc.tile_pool(name="resident", bufs=1))
-        turned_pool = ctx.enter_context(tc.tile_pool(name="turned", bufs=3))
+        turned_pool = ctx.enter_context(tc.tile_pool(name="turned", bufs=6))
         result_pool = ctx.enter_context(tc.tile_pool(name="result", bufs=8))
         psum = ctx.enter_context(tc.psum_pool(name="psum", bufs=PSUM_BANKS))
         ctx.enter_context(tc.manual_schedule())
@@ -167,15 +169,22 @@ def tile_attention_pa_kernel(
             for out_dram in (out_0, out_1)
             for j in range(CHUNKS)
         ]
+        planes = [
+            blank_planes(
+                nc, resident, nc.vector.memset if c < CHUNKS_AHEAD else nc.gpsimd.memset, sources[c][3]
+            )
+            for c in range(len(sources))
+        ]
         x_rows = []
         for b in range(BATCHES):
             rows = resident.tile([P, CHANNELS], BF16, name="x_rows_%d" % b, tag="x_rows_%d" % b)
             nc.sync.dma_start(out=rows[:], in_=x[b])
             x_rows.append(rows)
             if b == 0:
-                first_planes = load_chunk_scales(nc, resident, *sources[0])
-        chunks = [(load_chunk_words(nc, resident, *sources[0]), first_planes)]
-        chunks.extend([load_weight_chunk(nc, resident, *sources[c]) for c in range(1, CHUNKS_AHEAD)])
+                load_chunk_scales(nc, planes[0], *sources[0])
+        words = [load_chunk_words(nc, resident, *sources[0])]
+        for c in range(1, CHUNKS_AHEAD):
+            words.append(load_weight_chunk(nc, resident, planes[c], *sources[c]))
 
         cos_t, sin_t, neg_sin_t = rotation_factors(nc, resident, position)
 
@@ -184,7 +193,7 @@ def tile_attention_pa_kernel(
             for b in range(BATCHES)
         ]
 
-        def project_and_turn(b, words, planes, out_cols, first, width):
+        def project_and_turn(b, words, planes, first, width, result):
             codes, plane = x_mx[b]
             sums = psum.tile([P, width], F32, name="sums", tag="bank")
             for g in range(PASSES):
@@ -206,23 +215,33 @@ def tile_attention_pa_kernel(
             nc.scalar.activation(
                 out=turned[:, 1, :], in_=pairs[:, :, 0], func=ACT.Copy, scale=sin_t[:]
             )
-            result = result_pool.tile([P, width], F32, name="result")
             nc.vector.scalar_tensor_tensor(
-                out=result[:].rearrange("p (i e) -> p i e", e=2),
+                out=result.rearrange("p (i e) -> p i e", e=2),
                 in0=pairs,
                 scalar=cos_t[:],
                 in1=turned[:].rearrange("p e i -> p i e"),
                 op0=ALU.mult,
                 op1=ALU.add,
             )
-            nc.sync.dma_start(out=out_cols[b, :, first : first + width], in_=result[:])
 
-        last_bank = (len(sources) - 1, BATCHES - 1)
+        last_chunk = len(sources) - 1
+        store_widths = {
+            (last_chunk, BATCHES - 2): (2 * N_LAST, 2 * N_LAST),
+            (last_chunk, BATCHES - 1): (2 * N_LAST, N_LAST, N_LAST),
+        }
         for c in range(len(sources)):
             if c + CHUNKS_AHEAD < len(sources):
-                chunks.append(load_weight_chunk(nc, resident, *sources[c + CHUNKS_AHEAD]))
-            words, planes = chunks[c]
+                later = c + CHUNKS_AHEAD
+                words.append(load_weight_chunk(nc, resident, planes[later], *sources[later]))
             for b in range(BATCHES):
-                width = N_LAST if (c, b) == last_bank else N_CHUNK
-                for first in range(0, N_CHUNK, width):
-                    project_and_turn(b, words, planes, targets[c], first, width)
+                width = N_LAST if (c, b) in store_widths else N_CHUNK
+                store_first = 0
+                for store_width in store_widths.get((c, b), (N_CHUNK,)):
+                    store_cols = slice(store_first, store_first + store_width)
+                    result = result_pool.tile([P, store_width], F32, name="result")
+                    for first in range(0, store_width, width):
+                        project_and_turn(
+                            b, words[c], planes[c], store_first + first, width, result[:, first : first + width]
+                        )
+                    nc.sync.dma_start(out=targets[c][b, :, store_cols], in_=result[:])
+                    store_first += store_width

@@ -25,6 +25,7 @@ N_LAST = 128
 CHUNKS = CHANNELS // N_CHUNK
 PSUM_BANKS = 8
 CHUNKS_AHEAD = 3
+GROUPS = ((0,), (1,), (2, 3), (4, 5), (6, 7))
 QUADRANT = 32
 SCALE_ROWS = QUADRANT // 8
 
@@ -35,16 +36,15 @@ TWO_PI_LOW = 2.0 * math.pi - TWO_PI_HIGH
 ROUND_TO_WHOLE = 1.5 * 2.0**23
 
 
-def blank_planes(nc, pool, memset, label):
+def blank_planes(nc, pool, memset, width, label):
     planes = pool.tile(
-        [P, PASSES, N_CHUNK], U8, name="planes_" + label, tag="planes_" + label, align_bytes=64
+        [P, PASSES, width], U8, name="planes_" + label, tag="planes_" + label, align_bytes=64
     )
     memset(planes[:].bitcast(I32), 0)
     return planes
 
 
-def load_chunk_scales(nc, planes, words_dram, scales_dram, j, label):
-    n_cols = slice(N_CHUNK * j, N_CHUNK * (j + 1))
+def load_group_scales(nc, planes, scales_dram, n_cols):
     for r in range(SCALE_ROWS):
         nc.sync.dma_start(
             out=planes[r:P:QUADRANT].bitcast(I32),
@@ -54,22 +54,19 @@ def load_chunk_scales(nc, planes, words_dram, scales_dram, j, label):
         )
 
 
-def load_chunk_words(nc, pool, words_dram, scales_dram, j, label):
-    byte_cols = slice(2 * N_CHUNK * j, 2 * N_CHUNK * (j + 1))
+def load_group_words(nc, pool, words_dram, n_cols, label):
+    byte_cols = slice(2 * n_cols.start, 2 * n_cols.stop)
     words = []
     for g in range(PASSES):
         pass_label = "words_%s_%d" % (label, g)
-        pass_words = pool.tile([P, 2 * N_CHUNK], U8, name=pass_label, tag=pass_label, align_bytes=64)
+        pass_words = pool.tile(
+            [P, byte_cols.stop - byte_cols.start], U8, name=pass_label, tag=pass_label, align_bytes=64
+        )
         nc.sync.dma_start(
             out=pass_words[:].bitcast(I32), in_=words_dram[g, :, byte_cols].bitcast(I32)
         )
         words.append(pass_words)
     return words
-
-
-def load_weight_chunk(nc, pool, planes, words_dram, scales_dram, j, label):
-    load_chunk_scales(nc, planes, words_dram, scales_dram, j, label)
-    return load_chunk_words(nc, pool, words_dram, scales_dram, j, label)
 
 
 def rotation_factors(nc, pool, position):
@@ -156,14 +153,9 @@ def tile_attention_pa_kernel(
         identity = resident.tile([P, P], F32, name="identity")
         make_identity(nc, identity[:])
 
-        sources = [
-            (words_dram, scales_dram, j, "%s%d" % (name, j))
-            for name, words_dram, scales_dram in (
-                ("q", wq_words, wq_scales),
-                ("k", wk_words, wk_scales),
-            )
-            for j in range(CHUNKS)
-        ]
+        weights = ((wq_words, wq_scales), (wk_words, wk_scales))
+        n_chunks = len(weights) * CHUNKS
+        group_of = {c: i for i, group in enumerate(GROUPS) for c in group}
         targets = [
             out_dram.rearrange("b t h d -> b t (h d)")[:, :, N_CHUNK * j : N_CHUNK * (j + 1)]
             for out_dram in (out_0, out_1)
@@ -171,20 +163,40 @@ def tile_attention_pa_kernel(
         ]
         planes = [
             blank_planes(
-                nc, resident, nc.vector.memset if c < CHUNKS_AHEAD else nc.gpsimd.memset, sources[c][3]
+                nc,
+                resident,
+                nc.vector.memset if group[0] < CHUNKS_AHEAD else nc.gpsimd.memset,
+                N_CHUNK * len(group),
+                "%d" % group[0],
             )
-            for c in range(len(sources))
+            for group in GROUPS
         ]
+        words = {}
+
+        def weight_columns(i):
+            which, j = divmod(GROUPS[i][0], CHUNKS)
+            return weights[which], slice(N_CHUNK * j, N_CHUNK * (j + len(GROUPS[i])))
+
+        def load_scales(i):
+            weight, n_cols = weight_columns(i)
+            load_group_scales(nc, planes[i], weight[1], n_cols)
+
+        def load_words(i):
+            weight, n_cols = weight_columns(i)
+            words[i] = load_group_words(nc, resident, weight[0], n_cols, "%d" % GROUPS[i][0])
+
         x_rows = []
         for b in range(BATCHES):
             rows = resident.tile([P, CHANNELS], BF16, name="x_rows_%d" % b, tag="x_rows_%d" % b)
             nc.sync.dma_start(out=rows[:], in_=x[b])
             x_rows.append(rows)
             if b == 0:
-                load_chunk_scales(nc, planes[0], *sources[0])
-        words = [load_chunk_words(nc, resident, *sources[0])]
-        for c in range(1, CHUNKS_AHEAD):
-            words.append(load_weight_chunk(nc, resident, planes[c], *sources[c]))
+                load_scales(0)
+        load_words(0)
+        for i in range(1, len(GROUPS)):
+            if GROUPS[i][0] < CHUNKS_AHEAD:
+                load_scales(i)
+                load_words(i)
 
         cos_t, sin_t, neg_sin_t = rotation_factors(nc, resident, position)
 
@@ -224,15 +236,18 @@ def tile_attention_pa_kernel(
                 op1=ALU.add,
             )
 
-        last_chunk = len(sources) - 1
+        last_chunk = n_chunks - 1
         store_widths = {
             (last_chunk, BATCHES - 2): (2 * N_LAST, 2 * N_LAST),
             (last_chunk, BATCHES - 1): (2 * N_LAST, N_LAST, N_LAST),
         }
-        for c in range(len(sources)):
-            if c + CHUNKS_AHEAD < len(sources):
-                later = c + CHUNKS_AHEAD
-                words.append(load_weight_chunk(nc, resident, planes[later], *sources[later]))
+        for c in range(n_chunks):
+            for i in range(1, len(GROUPS)):
+                if GROUPS[i][0] == c + CHUNKS_AHEAD:
+                    load_scales(i)
+                    load_words(i)
+            i = group_of[c]
+            group_first = N_CHUNK * (c - GROUPS[i][0])
             for b in range(BATCHES):
                 width = N_LAST if (c, b) in store_widths else N_CHUNK
                 store_first = 0
@@ -241,7 +256,12 @@ def tile_attention_pa_kernel(
                     result = result_pool.tile([P, store_width], F32, name="result")
                     for first in range(0, store_width, width):
                         project_and_turn(
-                            b, words[c], planes[c], store_first + first, width, result[:, first : first + width]
+                            b,
+                            words[i],
+                            planes[i],
+                            group_first + store_first + first,
+                            width,
+                            result[:, first : first + width],
                         )
                     nc.sync.dma_start(out=targets[c][b, :, store_cols], in_=result[:])
                     store_first += store_width

@@ -16,6 +16,9 @@ ACT = mybir.ActivationFunctionType
 
 P = 128
 BATCHES = 4
+TENSOR_BATCHES = 3
+BLOCK = 32
+ROWS_A_LANE = P // BLOCK
 CHANNELS = 2048
 PACK = 4
 K_PASS = P * PACK
@@ -101,11 +104,22 @@ def rotation_factors(nc, pool, position):
     return cos_t, sin_t, neg_sin_t
 
 
-def quantise_batch(nc, pool, psum, x_rows, identity, label):
-    x_words = x_rows[:].bitcast(F32)
+def operand_tiles(pool, label):
     grouped = pool.tile(
         [P, PASSES, P, PACK], BF16, name="grouped_" + label, tag="grouped_" + label, align_bytes=64
     )
+    codes = pool.tile(
+        [P, PASSES * P], U32, name="codes_" + label, tag="codes_" + label, align_bytes=64
+    )
+    plane = pool.tile(
+        [P, PASSES * P], U8, name="plane_" + label, tag="plane_" + label, align_bytes=64
+    )
+    return grouped, codes, plane
+
+
+def flip_batch(nc, pool, psum, x_rows, identity, label):
+    x_words = x_rows[:].bitcast(F32)
+    grouped, codes, plane = operand_tiles(pool, label)
     grouped_words = grouped[:].bitcast(F32)
     words_per_pass = K_PASS // 2
     for first_pass in range(0, PASSES, 2):
@@ -123,18 +137,66 @@ def quantise_batch(nc, pool, psum, x_rows, identity, label):
             out=grouped_words[:, first_pass : first_pass + 2, :, :],
             in_=flipped[:].rearrange("p s u r -> p s r u"),
         )
-    codes = pool.tile(
-        [P, PASSES * P], U32, name="codes_" + label, tag="codes_" + label, align_bytes=64
-    )
-    plane = pool.tile(
-        [P, PASSES * P], U8, name="plane_" + label, tag="plane_" + label, align_bytes=64
-    )
+    return grouped, codes, plane
+
+
+def quantise_batch(nc, grouped, codes, plane):
     nc.vector.quantize_mx(
         out=codes[:].bitcast(FP8X4),
         scales=plane[:],
         in_=grouped[:].rearrange("p g r t -> p (g r t)"),
     )
-    return codes, plane
+
+
+def lane_tile(pool):
+    return pool.tile([P, ROWS_A_LANE * PASSES, P], BF16, name="lanes", align_bytes=64)
+
+
+def load_lanes(nc, lanes, x_batch, quadrant):
+    by_pass = x_batch.rearrange("r (g k) -> (r g) k", g=PASSES)
+    nc.sync.dma_start(
+        out=lanes[QUADRANT * quadrant : QUADRANT * (quadrant + 1)],
+        in_=by_pass[:, P * quadrant : P * (quadrant + 1)].rearrange("(j q) e -> j q e", j=QUADRANT),
+    )
+
+
+def vector_flip_steps(nc, pool, lanes, grouped, codes, plane):
+    raw = lanes[:].bitcast(F32).rearrange("p (s g) (m u) -> p g s u m", g=PASSES, u=2)
+    blocks = 2 * ROWS_A_LANE
+    parted = pool.tile([P, PASSES, blocks * BLOCK], F32, name="parted", align_bytes=64)
+    around = pool.tile([P, PASSES, blocks * BLOCK], F32, name="around", align_bytes=64)
+    grouped_words = grouped[:].bitcast(F32).rearrange("p g r u -> p g (r u)")
+
+    def sort(half):
+        for g in range(2 * half, 2 * half + 2):
+            nc.scalar.copy(
+                out=parted[:, g, :].rearrange("p (s u m) -> p s u m", u=2, m=BLOCK),
+                in_=raw[:, g],
+            )
+
+    def turn(half):
+        passes = slice(2 * half, 2 * half + 2)
+        nc.vector.transpose(
+            out=around[:, passes, :].rearrange("p g w -> p (g w)"),
+            in_=parted[:, passes, :].rearrange("p g w -> p (g w)"),
+        )
+
+    def gather(half):
+        passes = slice(2 * half, 2 * half + 2)
+        nc.vector.tensor_copy(
+            out=grouped_words[:, passes, :].rearrange("p g (j q) -> p g j q", j=BLOCK),
+            in_=around[:, passes, :].rearrange("p g (q j) -> p g j q", j=BLOCK),
+        )
+
+    def quantise(half):
+        cols = slice(2 * P * half, 2 * P * (half + 1))
+        nc.vector.quantize_mx(
+            out=codes[:, cols].bitcast(FP8X4),
+            scales=plane[:, cols],
+            in_=grouped[:, 2 * half : 2 * half + 2].rearrange("p g r t -> p (g r t)"),
+        )
+
+    return sort, turn, gather, quantise
 
 
 def tile_attention_pa_kernel(
@@ -144,7 +206,7 @@ def tile_attention_pa_kernel(
     with ExitStack() as ctx:
         resident = ctx.enter_context(tc.tile_pool(name="resident", bufs=1))
         turned_pool = ctx.enter_context(tc.tile_pool(name="turned", bufs=6))
-        result_pool = ctx.enter_context(tc.tile_pool(name="result", bufs=8))
+        result_pool = ctx.enter_context(tc.tile_pool(name="result", bufs=12))
         psum = ctx.enter_context(tc.psum_pool(name="psum", bufs=PSUM_BANKS))
         ctx.enter_context(tc.manual_schedule())
 
@@ -186,7 +248,7 @@ def tile_attention_pa_kernel(
             words[i] = load_group_words(nc, resident, weight[0], n_cols, "%d" % GROUPS[i][0])
 
         x_rows = []
-        for b in range(BATCHES):
+        for b in range(TENSOR_BATCHES):
             rows = resident.tile([P, CHANNELS], BF16, name="x_rows_%d" % b, tag="x_rows_%d" % b)
             nc.sync.dma_start(out=rows[:], in_=x[b])
             x_rows.append(rows)
@@ -200,10 +262,29 @@ def tile_attention_pa_kernel(
 
         cos_t, sin_t, neg_sin_t = rotation_factors(nc, resident, position)
 
-        x_mx = [
-            quantise_batch(nc, resident, psum, x_rows[b], identity, "%d" % b)
-            for b in range(BATCHES)
-        ]
+        operands = []
+        for b in range(TENSOR_BATCHES):
+            operands.append(flip_batch(nc, resident, psum, x_rows[b], identity, "%d" % b))
+            if b > 0:
+                quantise_batch(nc, *operands[b - 1])
+        quantise_batch(nc, *operands[-1])
+        x_mx = [(codes, plane) for grouped, codes, plane in operands]
+        lanes = lane_tile(resident)
+        grouped, codes, plane = operand_tiles(resident, "last")
+        x_mx.append((codes, plane))
+        sort, turn, gather, quantise = vector_flip_steps(nc, resident, lanes, grouped, codes, plane)
+        last_batch = BATCHES - 1
+        lane_loads = {1: 0, 2: 1, 5: 2, 6: 3}
+        steps_behind = {
+            14: (sort, 0),
+            15: (sort, 1),
+            16: (turn, 0),
+            17: (turn, 1),
+            18: (gather, 0),
+            19: (gather, 1),
+            20: (quantise, 0),
+            21: (quantise, 1),
+        }
 
         def project_and_turn(b, words, planes, first, width, result):
             codes, plane = x_mx[b]
@@ -238,30 +319,36 @@ def tile_attention_pa_kernel(
 
         last_chunk = n_chunks - 1
         store_widths = {
-            (last_chunk, BATCHES - 2): (2 * N_LAST, 2 * N_LAST),
-            (last_chunk, BATCHES - 1): (2 * N_LAST, N_LAST, N_LAST),
+            (last_chunk - 1, last_batch): (2 * N_LAST, 2 * N_LAST),
+            (last_chunk, last_batch): (2 * N_LAST, N_LAST, N_LAST),
         }
-        for c in range(n_chunks):
+        units = [(c, b) for c in range(n_chunks) for b in range(TENSOR_BATCHES)]
+        units += [(c, last_batch) for c in range(n_chunks)]
+        for unit, (c, b) in enumerate(units):
             for i in range(1, len(GROUPS)):
-                if GROUPS[i][0] == c + CHUNKS_AHEAD:
+                if b == 0 and GROUPS[i][0] == c + CHUNKS_AHEAD:
                     load_scales(i)
                     load_words(i)
+            if unit in lane_loads:
+                load_lanes(nc, lanes, x[last_batch], lane_loads[unit])
             i = group_of[c]
             group_first = N_CHUNK * (c - GROUPS[i][0])
-            for b in range(BATCHES):
-                width = N_LAST if (c, b) in store_widths else N_CHUNK
-                store_first = 0
-                for store_width in store_widths.get((c, b), (N_CHUNK,)):
-                    store_cols = slice(store_first, store_first + store_width)
-                    result = result_pool.tile([P, store_width], F32, name="result")
-                    for first in range(0, store_width, width):
-                        project_and_turn(
-                            b,
-                            words[i],
-                            planes[i],
-                            group_first + store_first + first,
-                            width,
-                            result[:, first : first + width],
-                        )
-                    nc.sync.dma_start(out=targets[c][b, :, store_cols], in_=result[:])
-                    store_first += store_width
+            width = N_LAST if (c, b) in store_widths else N_CHUNK
+            store_first = 0
+            for store_width in store_widths.get((c, b), (N_CHUNK,)):
+                store_cols = slice(store_first, store_first + store_width)
+                result = result_pool.tile([P, store_width], F32, name="result")
+                for first in range(0, store_width, width):
+                    project_and_turn(
+                        b,
+                        words[i],
+                        planes[i],
+                        group_first + store_first + first,
+                        width,
+                        result[:, first : first + width],
+                    )
+                nc.sync.dma_start(out=targets[c][b, :, store_cols], in_=result[:])
+                store_first += store_width
+            if unit in steps_behind:
+                step, half = steps_behind[unit]
+                step(half)

@@ -29,6 +29,7 @@ CHUNKS = CHANNELS // N_CHUNK
 PSUM_BANKS = 8
 CHUNKS_AHEAD = 3
 GROUPS = ((0,), (1,), (2, 3), (4, 5), (6, 7))
+BYTES_A_WORD_DMA = 2048
 QUADRANT = 32
 SCALE_ROWS = QUADRANT // 8
 
@@ -59,16 +60,19 @@ def load_group_scales(nc, planes, scales_dram, n_cols):
 
 def load_group_words(nc, pool, words_dram, n_cols, label):
     byte_cols = slice(2 * n_cols.start, 2 * n_cols.stop)
+    bytes_a_pass = byte_cols.stop - byte_cols.start
+    passes_a_dma = BYTES_A_WORD_DMA // bytes_a_pass
     words = []
-    for g in range(PASSES):
-        pass_label = "words_%s_%d" % (label, g)
-        pass_words = pool.tile(
-            [P, byte_cols.stop - byte_cols.start], U8, name=pass_label, tag=pass_label, align_bytes=64
+    for g in range(0, PASSES, passes_a_dma):
+        tile_label = "words_%s_%d" % (label, g)
+        some_words = pool.tile(
+            [P, passes_a_dma, bytes_a_pass], U8, name=tile_label, tag=tile_label, align_bytes=64
         )
         nc.sync.dma_start(
-            out=pass_words[:].bitcast(I32), in_=words_dram[g, :, byte_cols].bitcast(I32)
+            out=some_words[:].bitcast(I32),
+            in_=words_dram[g : g + passes_a_dma, :, byte_cols].rearrange("g p n -> p g n").bitcast(I32),
         )
-        words.append(pass_words)
+        words.extend([some_words[:, s] for s in range(passes_a_dma)])
     return words
 
 
@@ -274,16 +278,16 @@ def tile_attention_pa_kernel(
         x_mx.append((codes, plane))
         sort, turn, gather, quantise = vector_flip_steps(nc, resident, lanes, grouped, codes, plane)
         last_batch = BATCHES - 1
-        lane_loads = {1: 0, 2: 1, 5: 2, 6: 3}
+        lane_loads = {1: 0, 2: 1, 4: 2, 5: 3}
         steps_behind = {
-            14: (sort, 0),
-            15: (sort, 1),
-            16: (turn, 0),
-            17: (turn, 1),
-            18: (gather, 0),
-            19: (gather, 1),
-            20: (quantise, 0),
-            21: (quantise, 1),
+            10: (sort, 0),
+            11: (sort, 1),
+            12: (turn, 0),
+            13: (turn, 1),
+            14: (gather, 0),
+            15: (gather, 1),
+            16: (quantise, 0),
+            17: (quantise, 1),
         }
 
         def project_and_turn(b, words, planes, first, width, result):

import math
from contextlib import ExitStack

import concourse.mybir as mybir
from concourse.masks import make_identity

F32 = mybir.dt.float32
BF16 = mybir.dt.bfloat16
I32 = mybir.dt.int32
U32 = mybir.dt.uint32
U8 = mybir.dt.uint8
FP8X4 = mybir.dt.float8_e4m3fn_x4
FP4X4 = mybir.dt.float4_e2m1fn_x4
ALU = mybir.AluOpType
ACT = mybir.ActivationFunctionType

P = 128
BATCHES = 4
TENSOR_BATCHES = 3
BLOCK = 32
ROWS_A_LANE = P // BLOCK
CHANNELS = 2048
PACK = 4
K_PASS = P * PACK
PASSES = CHANNELS // K_PASS
N_CHUNK = 512
N_LAST = 128
CHUNKS = CHANNELS // N_CHUNK
PSUM_BANKS = 8
CHUNKS_AHEAD = 3
GROUPS = ((0,), (1,), (2, 3), (4, 5), (6, 7))
BYTES_A_WORD_DMA = 2048
QUADRANT = 32
SCALE_ROWS = QUADRANT // 8

FLOPS = 2 * 2 * BATCHES * P * CHANNELS * CHANNELS

TWO_PI_HIGH = 6.28125
TWO_PI_LOW = 2.0 * math.pi - TWO_PI_HIGH
ROUND_TO_WHOLE = 1.5 * 2.0**23


def blank_planes(nc, pool, memset, width, label):
    planes = pool.tile(
        [P, PASSES, width], U8, name="planes_" + label, tag="planes_" + label, align_bytes=64
    )
    memset(planes[:].bitcast(I32), 0)
    return planes


def load_group_scales(nc, planes, scales_dram, n_cols):
    for r in range(SCALE_ROWS):
        nc.sync.dma_start(
            out=planes[r:P:QUADRANT].bitcast(I32),
            in_=scales_dram[:, r : P // 8 : SCALE_ROWS, n_cols]
            .rearrange("g q n -> q g n")
            .bitcast(I32),
        )


def load_group_words(nc, pool, words_dram, n_cols, label):
    byte_cols = slice(2 * n_cols.start, 2 * n_cols.stop)
    bytes_a_pass = byte_cols.stop - byte_cols.start
    passes_a_dma = BYTES_A_WORD_DMA // bytes_a_pass
    words = []
    for g in range(0, PASSES, passes_a_dma):
        tile_label = "words_%s_%d" % (label, g)
        some_words = pool.tile(
            [P, passes_a_dma, bytes_a_pass], U8, name=tile_label, tag=tile_label, align_bytes=64
        )
        nc.sync.dma_start(
            out=some_words[:].bitcast(I32),
            in_=words_dram[g : g + passes_a_dma, :, byte_cols].rearrange("g p n -> p g n").bitcast(I32),
        )
        words.extend([some_words[:, s] for s in range(passes_a_dma)])
    return words


def rotation_factors(nc, pool, position):
    angle = pool.tile([P, 1], F32, name="angle")
    turns = pool.tile([P, 1], F32, name="turns")
    quarter_less = pool.tile([P, 1], F32, name="quarter_less")
    cos_t = pool.tile([P, 1], F32, name="cos_t")
    sin_t = pool.tile([P, 1], F32, name="sin_t")
    neg_sin_t = pool.tile([P, 1], F32, name="neg_sin_t")

    nc.vector.tensor_copy(out=angle[:], in_=position[:])
    nc.vector.tensor_scalar(
        out=turns[:], in0=angle[:], scalar1=1.0 / (2.0 * math.pi), scalar2=ROUND_TO_WHOLE,
        op0=ALU.mult, op1=ALU.add,
    )
    nc.vector.tensor_scalar(
        out=turns[:], in0=turns[:], scalar1=ROUND_TO_WHOLE, scalar2=None, op0=ALU.subtract
    )
    for part in (TWO_PI_HIGH, TWO_PI_LOW):
        nc.vector.scalar_tensor_tensor(
            out=angle[:], in0=turns[:], scalar=-part, in1=angle[:], op0=ALU.mult, op1=ALU.add
        )
    nc.vector.scalar_tensor_tensor(
        out=quarter_less[:], in0=angle[:], scalar=-1.0, in1=angle[:], op0=ALU.mult, op1=ALU.min
    )
    nc.vector.tensor_scalar(
        out=quarter_less[:], in0=quarter_less[:], scalar1=0.5 * math.pi, scalar2=None, op0=ALU.add
    )
    nc.scalar.activation(out=sin_t[:], in_=angle[:], func=ACT.Sin)
    nc.scalar.activation(out=neg_sin_t[:], in_=angle[:], func=ACT.Sin, scale=-1.0)
    nc.scalar.activation(out=cos_t[:], in_=quarter_less[:], func=ACT.Sin)
    return cos_t, sin_t, neg_sin_t


def operand_tiles(pool, label):
    grouped = pool.tile(
        [P, PASSES, P, PACK], BF16, name="grouped_" + label, tag="grouped_" + label, align_bytes=64
    )
    codes = pool.tile(
        [P, PASSES * P], U32, name="codes_" + label, tag="codes_" + label, align_bytes=64
    )
    plane = pool.tile(
        [P, PASSES * P], U8, name="plane_" + label, tag="plane_" + label, align_bytes=64
    )
    return grouped, codes, plane


def flip_batch(nc, pool, psum, x_rows, identity, label):
    x_words = x_rows[:].bitcast(F32)
    grouped, codes, plane = operand_tiles(pool, label)
    grouped_words = grouped[:].bitcast(F32)
    words_per_pass = K_PASS // 2
    for first_pass in range(0, PASSES, 2):
        flipped = psum.tile([P, 2, 2, P], F32, name="flipped", tag="bank")
        for s in range(2):
            for u in range(2):
                start = words_per_pass * (first_pass + s)
                nc.tensor.transpose(
                    flipped[:, s, u, :],
                    x_words[:, start + u : start + words_per_pass : 2],
                    identity[:],
                )
        copy_out = nc.vector.tensor_copy if first_pass == 0 else nc.scalar.copy
        copy_out(
            out=grouped_words[:, first_pass : first_pass + 2, :, :],
            in_=flipped[:].rearrange("p s u r -> p s r u"),
        )
    return grouped, codes, plane


def quantise_batch(nc, grouped, codes, plane):
    nc.vector.quantize_mx(
        out=codes[:].bitcast(FP8X4),
        scales=plane[:],
        in_=grouped[:].rearrange("p g r t -> p (g r t)"),
    )


def lane_tile(pool):
    return pool.tile([P, ROWS_A_LANE * PASSES, P], BF16, name="lanes", align_bytes=64)


def load_lanes(nc, lanes, x_batch, quadrant):
    by_pass = x_batch.rearrange("r (g k) -> (r g) k", g=PASSES)
    nc.sync.dma_start(
        out=lanes[QUADRANT * quadrant : QUADRANT * (quadrant + 1)],
        in_=by_pass[:, P * quadrant : P * (quadrant + 1)].rearrange("(j q) e -> j q e", j=QUADRANT),
    )


def vector_flip_steps(nc, pool, lanes, grouped, codes, plane):
    raw = lanes[:].bitcast(F32).rearrange("p (s g) (m u) -> p g s u m", g=PASSES, u=2)
    blocks = 2 * ROWS_A_LANE
    parted = pool.tile([P, PASSES, blocks * BLOCK], F32, name="parted", align_bytes=64)
    around = pool.tile([P, PASSES, blocks * BLOCK], F32, name="around", align_bytes=64)
    grouped_words = grouped[:].bitcast(F32).rearrange("p g r u -> p g (r u)")

    def sort(half):
        for g in range(2 * half, 2 * half + 2):
            nc.scalar.copy(
                out=parted[:, g, :].rearrange("p (s u m) -> p s u m", u=2, m=BLOCK),
                in_=raw[:, g],
            )

    def turn(half):
        passes = slice(2 * half, 2 * half + 2)
        nc.vector.transpose(
            out=around[:, passes, :].rearrange("p g w -> p (g w)"),
            in_=parted[:, passes, :].rearrange("p g w -> p (g w)"),
        )

    def gather(half):
        passes = slice(2 * half, 2 * half + 2)
        nc.vector.tensor_copy(
            out=grouped_words[:, passes, :].rearrange("p g (j q) -> p g j q", j=BLOCK),
            in_=around[:, passes, :].rearrange("p g (q j) -> p g j q", j=BLOCK),
        )

    def quantise(half):
        cols = slice(2 * P * half, 2 * P * (half + 1))
        nc.vector.quantize_mx(
            out=codes[:, cols].bitcast(FP8X4),
            scales=plane[:, cols],
            in_=grouped[:, 2 * half : 2 * half + 2].rearrange("p g r t -> p (g r t)"),
        )

    return sort, turn, gather, quantise


def tile_attention_pa_kernel(
    tc, x, wq_words, wq_scales, wk_words, wk_scales, out_0, out_1
):
    nc = tc.nc
    with ExitStack() as ctx:
        resident = ctx.enter_context(tc.tile_pool(name="resident", bufs=1))
        turned_pool = ctx.enter_context(tc.tile_pool(name="turned", bufs=6))
        result_pool = ctx.enter_context(tc.tile_pool(name="result", bufs=12))
        psum = ctx.enter_context(tc.psum_pool(name="psum", bufs=PSUM_BANKS))
        ctx.enter_context(tc.manual_schedule())

        position = resident.tile([P, 1], I32, name="position")
        nc.gpsimd.iota(position[:], pattern=[[0, 1]], base=0, channel_multiplier=1)
        identity = resident.tile([P, P], F32, name="identity")
        make_identity(nc, identity[:])

        weights = ((wq_words, wq_scales), (wk_words, wk_scales))
        n_chunks = len(weights) * CHUNKS
        group_of = {c: i for i, group in enumerate(GROUPS) for c in group}
        targets = [
            out_dram.rearrange("b t h d -> b t (h d)")[:, :, N_CHUNK * j : N_CHUNK * (j + 1)]
            for out_dram in (out_0, out_1)
            for j in range(CHUNKS)
        ]
        planes = [
            blank_planes(
                nc,
                resident,
                nc.vector.memset if group[0] < CHUNKS_AHEAD else nc.gpsimd.memset,
                N_CHUNK * len(group),
                "%d" % group[0],
            )
            for group in GROUPS
        ]
        words = {}

        def weight_columns(i):
            which, j = divmod(GROUPS[i][0], CHUNKS)
            return weights[which], slice(N_CHUNK * j, N_CHUNK * (j + len(GROUPS[i])))

        def load_scales(i):
            weight, n_cols = weight_columns(i)
            load_group_scales(nc, planes[i], weight[1], n_cols)

        def load_words(i):
            weight, n_cols = weight_columns(i)
            words[i] = load_group_words(nc, resident, weight[0], n_cols, "%d" % GROUPS[i][0])

        x_rows = []
        for b in range(TENSOR_BATCHES):
            rows = resident.tile([P, CHANNELS], BF16, name="x_rows_%d" % b, tag="x_rows_%d" % b)
            nc.sync.dma_start(out=rows[:], in_=x[b])
            x_rows.append(rows)
            if b == 0:
                load_scales(0)
        load_words(0)
        for i in range(1, len(GROUPS)):
            if GROUPS[i][0] < CHUNKS_AHEAD:
                load_scales(i)
                load_words(i)

        cos_t, sin_t, neg_sin_t = rotation_factors(nc, resident, position)

        operands = []
        for b in range(TENSOR_BATCHES):
            operands.append(flip_batch(nc, resident, psum, x_rows[b], identity, "%d" % b))
            if b > 0:
                quantise_batch(nc, *operands[b - 1])
        quantise_batch(nc, *operands[-1])
        x_mx = [(codes, plane) for grouped, codes, plane in operands]
        lanes = lane_tile(resident)
        grouped, codes, plane = operand_tiles(resident, "last")
        x_mx.append((codes, plane))
        sort, turn, gather, quantise = vector_flip_steps(nc, resident, lanes, grouped, codes, plane)
        last_batch = BATCHES - 1
        lane_loads = {1: 0, 2: 1, 4: 2, 5: 3}
        steps_behind = {
            10: (sort, 0),
            11: (sort, 1),
            12: (turn, 0),
            13: (turn, 1),
            14: (gather, 0),
            15: (gather, 1),
            16: (quantise, 0),
            17: (quantise, 1),
        }

        def project_and_turn(b, words, planes, first, width, result):
            codes, plane = x_mx[b]
            sums = psum.tile([P, width], F32, name="sums", tag="bank")
            for g in range(PASSES):
                positions = slice(P * g, P * (g + 1))
                nc.tensor.matmul_mx(
                    out=sums[:],
                    lhsT=codes[:, positions].bitcast(FP8X4),
                    lhsT_scale=plane[:, positions],
                    rhs=words[g][:, 2 * first : 2 * (first + width)].bitcast(FP4X4),
                    rhs_scale=planes[:, g, first : first + width],
                    start=(g == 0),
                    stop=(g == PASSES - 1),
                )
            pairs = sums[:].rearrange("p (i e) -> p i e", e=2)
            turned = turned_pool.tile([P, 2, width // 2], F32, name="turned")
            nc.scalar.activation(
                out=turned[:, 0, :], in_=pairs[:, :, 1], func=ACT.Copy, scale=neg_sin_t[:]
            )
            nc.scalar.activation(
                out=turned[:, 1, :], in_=pairs[:, :, 0], func=ACT.Copy, scale=sin_t[:]
            )
            nc.vector.scalar_tensor_tensor(
                out=result.rearrange("p (i e) -> p i e", e=2),
                in0=pairs,
                scalar=cos_t[:],
                in1=turned[:].rearrange("p e i -> p i e"),
                op0=ALU.mult,
                op1=ALU.add,
            )

        last_chunk = n_chunks - 1
        store_widths = {
            (last_chunk - 1, last_batch): (2 * N_LAST, 2 * N_LAST),
            (last_chunk, last_batch): (2 * N_LAST, N_LAST, N_LAST),
        }
        units = [(c, b) for c in range(n_chunks) for b in range(TENSOR_BATCHES)]
        units += [(c, last_batch) for c in range(n_chunks)]
        for unit, (c, b) in enumerate(units):
            for i in range(1, len(GROUPS)):
                if b == 0 and GROUPS[i][0] == c + CHUNKS_AHEAD:
                    load_scales(i)
                    load_words(i)
            if unit in lane_loads:
                load_lanes(nc, lanes, x[last_batch], lane_loads[unit])
            i = group_of[c]
            group_first = N_CHUNK * (c - GROUPS[i][0])
            width = N_LAST if (c, b) in store_widths else N_CHUNK
            store_first = 0
            for store_width in store_widths.get((c, b), (N_CHUNK,)):
                store_cols = slice(store_first, store_first + store_width)
                result = result_pool.tile([P, store_width], F32, name="result")
                for first in range(0, store_width, width):
                    project_and_turn(
                        b,
                        words[i],
                        planes[i],
                        group_first + store_first + first,
                        width,
                        result[:, first : first + width],
                    )
                nc.sync.dma_start(out=targets[c][b, :, store_cols], in_=result[:])
                store_first += store_width
            if unit in steps_behind:
                step, half = steps_behind[unit]
                step(half)
